import numpy as np
import ml_dtypes


def mxq(x, axis, fmt="e4m3"):
    dtype, down = {"e4m3": (ml_dtypes.float8_e4m3fn, 7), "e5m2": (ml_dtypes.float8_e5m2, 14)}[fmt]
    v = np.moveaxis(np.asarray(x, np.float32).astype(ml_dtypes.bfloat16).astype(np.float64), axis, -1)
    blocks = v.reshape(v.shape[:-1] + (-1, 32))
    amax = np.abs(blocks).max(-1, keepdims=True)
    byte = np.maximum(np.where(amax > 0, np.frexp(amax)[1] - 1 + 127, 0) - down, 1)
    scale = np.exp2(byte - 127.0)
    codes = (blocks / scale).astype(np.float32).astype(dtype).astype(np.float64)
    return np.moveaxis((codes * scale).reshape(v.shape), -1, axis)


WIDE = False


def mx_kscale(k):
    if not WIDE:
        return np.ones(k)
    levels = np.array([10, -10, 5, -5, 0])
    a = np.random.permutation(np.resize(levels, k // 512 * 4)).reshape(k // 512, 4)
    idx = np.arange(k)
    return np.exp2(a[idx // 512, idx % 128 // 32])


BF16 = ml_dtypes.bfloat16


def bf(x):
    return np.asarray(x, np.float32).astype(BF16)


def f64(x):
    return np.asarray(x).astype(np.float64)


B, N, F, O, E, K = 4, 512, 512, 64, 16, 3


def setup_inputs():
    s = mx_kscale(F)
    return {"x_g": bf(np.random.standard_normal((B, K, N, F)) * s),
            "emb": bf(np.random.standard_normal((B, N, E))),
            "weights_pool": bf(np.random.standard_normal((E, K, F, O)) * 0.5 / np.sqrt(K * F) / s[:, None]),
            "bias_pool": bf(np.random.standard_normal((E, O)) * 0.3)}


def reference(x_g, emb, weights_pool, bias_pool):
    xg, w, g = f64(x_g), f64(weights_pool), f64(emb)
    z = 0.0
    for k in range(K):
        wk = w[:, k].transpose(1, 0, 2).reshape(F, E * O)
        z = z + (mxq(xg[:, k], 2, "e4m3") @ mxq(wk, 0, "e4m3"))
    z = z.reshape(B, N, E, O)
    out = (g[:, :, :, None] * z).sum(2)
    return out + (g[:, :, :, None] * f64(bias_pool)[None, None, :, :]).sum(2)

@@ -1,0 +1,180 @@
+from contextlib import ExitStack
+
+import concourse.mybir as mybir
+from concourse.masks import make_identity
+
+BF16 = mybir.dt.bfloat16
+F32 = mybir.dt.float32
+U32 = mybir.dt.uint32
+U8 = mybir.dt.uint8
+FP8X4 = mybir.dt.float8_e4m3fn_x4
+MULT = mybir.AluOpType.mult
+ADD = mybir.AluOpType.add
+
+P = 128
+PACK = 4
+BATCH, ORDERS, NODES, FEAT = 4, 3, 512, 512
+SETS, OUT = 16, 64
+TILES = NODES // P
+HALVES = 2
+WORDS = FEAT // 2
+ROUND_SETS = 8
+ROUNDS = SETS // ROUND_SETS
+ROUND_COLS = ROUND_SETS * OUT
+VECTOR_SETS = 5
+
+FLOPS = 2 * BATCH * NODES * ORDERS * FEAT * SETS * OUT
+
+
+def tile_dygcn_pb_kernel(tc, x_g, emb, weights_pool, bias_pool, out):
+    nc = tc.nc
+    with ExitStack() as ctx:
+        keep = ctx.enter_context(tc.tile_pool(name="keep", bufs=1))
+        stage = ctx.enter_context(tc.tile_pool(name="stage", bufs=3))
+        psum_x = ctx.enter_context(tc.psum_pool(name="psum_x", bufs=4))
+        psum_z = ctx.enter_context(tc.psum_pool(name="psum_z", bufs=4))
+
+        x_raw = [keep.tile([P, ORDERS * TILES * FEAT], BF16, name="x_raw%d" % b) for b in range(BATCH)]
+        w_raw = [keep.tile([P, ORDERS, ROUND_SETS, PACK * OUT], BF16, name="w_raw%d" % r) for r in range(ROUNDS)]
+        x_codes = keep.tile([P, BATCH * ORDERS, TILES * P], U32, align_bytes=64)
+        x_scales = keep.tile([P, BATCH * ORDERS, TILES * P], U8, align_bytes=64)
+        w_codes = keep.tile([P, ROUNDS * ORDERS, ROUND_COLS], U32, align_bytes=64)
+        w_scales = keep.tile([P, ROUNDS * ORDERS, ROUND_COLS], U8, align_bytes=64)
+        acc = keep.tile([P, BATCH * TILES, OUT], F32)
+
+        def load_x(b, k):
+            nc.sync.dma_start(
+                out=x_raw[b][:, k * TILES * FEAT : (k + 1) * TILES * FEAT],
+                in_=x_g[b, k].rearrange("(p t) f -> p (t f)", t=TILES),
+            )
+
+        def load_w(r, k):
+            for u in range(HALVES):
+                nc.sync.dma_start(
+                    out=w_raw[r][:, k, :, u * 2 * OUT : (u + 1) * 2 * OUT],
+                    in_=weights_pool[
+                        r * ROUND_SETS : (r + 1) * ROUND_SETS, k, u * 2 * P : (u + 1) * 2 * P, :
+                    ].rearrange("e (p c) o -> p e (c o)", c=2),
+                )
+
+        for k in range(ORDERS):
+            load_w(0, k)
+            load_x(0, k)
+        for b in range(1, BATCH):
+            for k in range(ORDERS):
+                load_x(b, k)
+        for r in range(1, ROUNDS):
+            for k in range(ORDERS):
+                load_w(r, k)
+
+        ident = keep.tile([P, P], F32)
+        make_identity(nc, ident[:])
+        emb_bf = keep.tile([P, BATCH, TILES * SETS], BF16)
+        nc.scalar.dma_start(out=emb_bf[:], in_=emb.rearrange("b (p t) e -> p b (t e)", t=TILES))
+        DIAG = P // SETS
+        bias_diag = keep.tile([P, DIAG * OUT], BF16)
+        nc.vector.memset(bias_diag[:], 0.0)
+        for d in range(DIAG):
+            nc.scalar.dma_start(
+                out=bias_diag[d * SETS : (d + 1) * SETS, d * OUT : (d + 1) * OUT], in_=bias_pool
+            )
+        emb_f32 = keep.tile([P, BATCH * TILES * SETS], F32)
+        nc.vector.tensor_copy(out=emb_f32[:], in_=emb_bf[:].rearrange("p b c -> p (b c)"))
+        GROUPS = BATCH * TILES // DIAG
+        emb_t_ps = psum_x.tile([P, GROUPS, P], F32, name="xt")
+        for g in range(GROUPS):
+            nc.tensor.transpose(emb_t_ps[:, g, :], emb_f32[:, g * P : (g + 1) * P], ident[:])
+        emb_t = keep.tile([P, GROUPS, P], BF16)
+        nc.vector.tensor_copy(out=emb_t[:], in_=emb_t_ps[:])
+        for g in range(GROUPS):
+            bias_ps = psum_z.tile([P, DIAG * OUT], F32, name="z")
+            nc.tensor.matmul(bias_ps[:], lhsT=emb_t[:, g, :], rhs=bias_diag[:], start=True, stop=True)
+            nc.scalar.copy(
+                out=acc[:, g * DIAG : (g + 1) * DIAG, :].rearrange("p d o -> p (d o)"), in_=bias_ps[:]
+            )
+
+        def prepare_w(r):
+            for k in range(ORDERS):
+                grouped = stage.tile([P, ROUND_COLS, PACK], BF16, align_bytes=64, name="w_grouped")
+                split = VECTOR_SETS * OUT
+                nc.vector.tensor_copy(
+                    out=grouped[:, :split, :].rearrange("p (e c i) j -> p e c j i", e=VECTOR_SETS, i=4),
+                    in_=w_raw[r][:, k, :VECTOR_SETS, :].rearrange("p e (j c i) -> p e c j i", j=PACK, i=4),
+                )
+                nc.scalar.copy(
+                    out=grouped[:, split:, :].rearrange("p (e o) j -> p e o j", o=OUT),
+                    in_=w_raw[r][:, k, VECTOR_SETS:, :].rearrange("p e (j o) -> p e o j", j=PACK),
+                )
+                nc.vector.quantize_mx(
+                    out=w_codes[:, r * ORDERS + k, :].bitcast(FP8X4),
+                    scales=w_scales[:, r * ORDERS + k, :],
+                    in_=grouped[:].rearrange("p c j -> p (c j)"),
+                )
+
+        def prepare_x(b):
+            x_words = x_raw[b][:].bitcast(F32)
+            for k in range(ORDERS):
+                grouped = stage.tile([P, TILES * P * PACK], BF16, align_bytes=64, name="x_grouped")
+                grouped_words = grouped[:].bitcast(F32).rearrange("p (t n u) -> p t n u", t=TILES, u=HALVES)
+                for pair in range(TILES // 2):
+                    xt = psum_x.tile([P, 2, HALVES, P], F32, name="xt")
+                    for i in range(2):
+                        row = (k * TILES + 2 * pair + i) * WORDS
+                        for u in range(HALVES):
+                            nc.tensor.transpose(
+                                xt[:, i, u, :], x_words[:, row + u * P : row + (u + 1) * P], ident[:]
+                            )
+                    nc.scalar.copy(
+                        out=grouped_words[:, 2 * pair : 2 * pair + 2, :, :],
+                        in_=xt[:].rearrange("p i u n -> p i n u"),
+                    )
+                nc.vector.quantize_mx(
+                    out=x_codes[:, b * ORDERS + k, :].bitcast(FP8X4),
+                    scales=x_scales[:, b * ORDERS + k, :],
+                    in_=grouped[:],
+                )
+
+        def node_tile_pair(r, b, pair):
+            tiles = (2 * pair, 2 * pair + 1)
+            banks = []
+            for t in tiles:
+                z = psum_z.tile([P, ROUND_COLS], F32, name="z")
+                banks.append(z)
+                for k in range(ORDERS):
+                    nc.tensor.matmul_mx(
+                        out=z[:],
+                        lhsT=x_codes[:, b * ORDERS + k, t * P : (t + 1) * P].bitcast(FP8X4),
+                        lhsT_scale=x_scales[:, b * ORDERS + k, t * P : (t + 1) * P],
+                        rhs=w_codes[:, r * ORDERS + k, :].bitcast(FP8X4),
+                        rhs_scale=w_scales[:, r * ORDERS + k, :],
+                        start=(k == 0),
+                        stop=(k == ORDERS - 1),
+                    )
+            for s in range(ROUND_SETS):
+                for t, z in zip(tiles, banks):
+                    row = b * TILES + t
+                    col = row * SETS + r * ROUND_SETS + s
+                    nc.vector.scalar_tensor_tensor(
+                        out=acc[:, row, :],
+                        in0=z[:, s * OUT : (s + 1) * OUT],
+                        scalar=emb_f32[:, col : col + 1],
+                        in1=acc[:, row, :],
+                        op0=MULT,
+                        op1=ADD,
+                    )
+
+        prepare_w(0)
+        prepare_x(0)
+        for r in range(ROUNDS):
+            for b in range(BATCH):
+                if r == 0 and b + 1 < BATCH:
+                    prepare_x(b + 1)
+                if r + 1 < ROUNDS and b == BATCH - 1:
+                    prepare_w(r + 1)
+                for pair in range(TILES // 2):
+                    node_tile_pair(r, b, pair)
+                if r == ROUNDS - 1:
+                    nc.sync.dma_start(
+                        out=out[b].rearrange("(p t) o -> p (t o)", t=TILES),
+                        in_=acc[:, b * TILES : (b + 1) * TILES, :].rearrange("p t o -> p (t o)"),
+                    )

@@ -16,12 +16,15 @@ PACK = 4
 BATCH, ORDERS, NODES, FEAT = 4, 3, 512, 512
 SETS, OUT = 16, 64
 TILES = NODES // P
+ROWS = BATCH * TILES
 HALVES = 2
 WORDS = FEAT // 2
-ROUND_SETS = 8
+BANK = 512
+ROUND_SETS = 4
 ROUNDS = SETS // ROUND_SETS
 ROUND_COLS = ROUND_SETS * OUT
-VECTOR_SETS = 5
+BANK_TILES = BANK // ROUND_COLS
+SLOTS = 2
 
 FLOPS = 2 * BATCH * NODES * ORDERS * FEAT * SETS * OUT
 
@@ -40,71 +43,74 @@ def tile_dygcn_pb_kernel(tc, x_g, emb, weights_pool, bias_pool, out):
         x_scales = keep.tile([P, BATCH * ORDERS, TILES * P], U8, align_bytes=64)
         w_codes = keep.tile([P, ROUNDS * ORDERS, ROUND_COLS], U32, align_bytes=64)
         w_scales = keep.tile([P, ROUNDS * ORDERS, ROUND_COLS], U8, align_bytes=64)
-        acc = keep.tile([P, BATCH * TILES, OUT], F32)
+        acc = keep.tile([P, SLOTS, ROWS, OUT], F32)
 
-        def load_x(b, k):
-            nc.sync.dma_start(
-                out=x_raw[b][:, k * TILES * FEAT : (k + 1) * TILES * FEAT],
-                in_=x_g[b, k].rearrange("(p t) f -> p (t f)", t=TILES),
-            )
-
-        def load_w(r, k):
-            for u in range(HALVES):
+        def load_x(b):
+            for k in range(ORDERS):
                 nc.sync.dma_start(
-                    out=w_raw[r][:, k, :, u * 2 * OUT : (u + 1) * 2 * OUT],
-                    in_=weights_pool[
-                        r * ROUND_SETS : (r + 1) * ROUND_SETS, k, u * 2 * P : (u + 1) * 2 * P, :
-                    ].rearrange("e (p c) o -> p e (c o)", c=2),
+                    out=x_raw[b][:, k * TILES * FEAT : (k + 1) * TILES * FEAT],
+                    in_=x_g[b, k].rearrange("(p t) f -> p (t f)", t=TILES),
                 )
 
-        for k in range(ORDERS):
-            load_w(0, k)
-            load_x(0, k)
+        def load_w(r):
+            for k in range(ORDERS):
+                for u in range(HALVES):
+                    nc.sync.dma_start(
+                        out=w_raw[r][:, k, :, u * 2 * OUT : (u + 1) * 2 * OUT],
+                        in_=weights_pool[
+                            r * ROUND_SETS : (r + 1) * ROUND_SETS, k, u * 2 * P : (u + 1) * 2 * P, :
+                        ].rearrange("e (p c) o -> p e (c o)", c=2),
+                    )
+
+        load_x(0)
+        load_w(0)
         for b in range(1, BATCH):
-            for k in range(ORDERS):
-                load_x(b, k)
+            load_x(b)
         for r in range(1, ROUNDS):
-            for k in range(ORDERS):
-                load_w(r, k)
+            load_w(r)
 
         ident = keep.tile([P, P], F32)
         make_identity(nc, ident[:])
         emb_bf = keep.tile([P, BATCH, TILES * SETS], BF16)
         nc.scalar.dma_start(out=emb_bf[:], in_=emb.rearrange("b (p t) e -> p b (t e)", t=TILES))
         DIAG = P // SETS
+        GROUPS = ROWS // DIAG
         bias_diag = keep.tile([P, DIAG * OUT], BF16)
         nc.vector.memset(bias_diag[:], 0.0)
         for d in range(DIAG):
             nc.scalar.dma_start(
                 out=bias_diag[d * SETS : (d + 1) * SETS, d * OUT : (d + 1) * OUT], in_=bias_pool
             )
-        emb_f32 = keep.tile([P, BATCH * TILES * SETS], F32)
+        nc.vector.memset(acc[:, 1, :, :], 0.0)
+        emb_f32 = keep.tile([P, ROWS * SETS], F32)
         nc.vector.tensor_copy(out=emb_f32[:], in_=emb_bf[:].rearrange("p b c -> p (b c)"))
-        GROUPS = BATCH * TILES // DIAG
         emb_t_ps = psum_x.tile([P, GROUPS, P], F32, name="xt")
         for g in range(GROUPS):
             nc.tensor.transpose(emb_t_ps[:, g, :], emb_f32[:, g * P : (g + 1) * P], ident[:])
         emb_t = keep.tile([P, GROUPS, P], BF16)
         nc.vector.tensor_copy(out=emb_t[:], in_=emb_t_ps[:])
-        for g in range(GROUPS):
-            bias_ps = psum_z.tile([P, DIAG * OUT], F32, name="z")
-            nc.tensor.matmul(bias_ps[:], lhsT=emb_t[:, g, :], rhs=bias_diag[:], start=True, stop=True)
-            nc.scalar.copy(
-                out=acc[:, g * DIAG : (g + 1) * DIAG, :].rearrange("p d o -> p (d o)"), in_=bias_ps[:]
-            )
+
+        def bias_term():
+            for g in range(GROUPS):
+                bias_ps = psum_z.tile([P, DIAG * OUT], F32, name="z")
+                nc.tensor.matmul(bias_ps[:], lhsT=emb_t[:, g, :], rhs=bias_diag[:], start=True, stop=True)
+                nc.scalar.copy(
+                    out=acc[:, 0, g * DIAG : (g + 1) * DIAG, :].rearrange("p d o -> p (d o)"), in_=bias_ps[:]
+                )
 
         def prepare_w(r):
             for k in range(ORDERS):
                 grouped = stage.tile([P, ROUND_COLS, PACK], BF16, align_bytes=64, name="w_grouped")
-                split = VECTOR_SETS * OUT
-                nc.vector.tensor_copy(
-                    out=grouped[:, :split, :].rearrange("p (e c i) j -> p e c j i", e=VECTOR_SETS, i=4),
-                    in_=w_raw[r][:, k, :VECTOR_SETS, :].rearrange("p e (j c i) -> p e c j i", j=PACK, i=4),
-                )
-                nc.scalar.copy(
-                    out=grouped[:, split:, :].rearrange("p (e o) j -> p e o j", o=OUT),
-                    in_=w_raw[r][:, k, VECTOR_SETS:, :].rearrange("p e (j o) -> p e o j", j=PACK),
-                )
+                if k == 0:
+                    nc.scalar.copy(
+                        out=grouped[:].rearrange("p (e o) j -> p e o j", o=OUT),
+                        in_=w_raw[r][:, k, :, :].rearrange("p e (j o) -> p e o j", j=PACK),
+                    )
+                else:
+                    nc.vector.tensor_copy(
+                        out=grouped[:].rearrange("p (e c i) j -> p e c j i", e=ROUND_SETS, i=4),
+                        in_=w_raw[r][:, k, :, :].rearrange("p e (j c i) -> p e c j i", j=PACK, i=4),
+                    )
                 nc.vector.quantize_mx(
                     out=w_codes[:, r * ORDERS + k, :].bitcast(FP8X4),
                     scales=w_scales[:, r * ORDERS + k, :],
@@ -134,47 +140,54 @@ def tile_dygcn_pb_kernel(tc, x_g, emb, weights_pool, bias_pool, out):
                     in_=grouped[:],
                 )
 
-        def node_tile_pair(r, b, pair):
-            tiles = (2 * pair, 2 * pair + 1)
+        def batch_round(r, b):
             banks = []
-            for t in tiles:
-                z = psum_z.tile([P, ROUND_COLS], F32, name="z")
+            for j in range(TILES // BANK_TILES):
+                z = psum_z.tile([P, BANK_TILES, ROUND_COLS], F32, name="z")
                 banks.append(z)
-                for k in range(ORDERS):
-                    nc.tensor.matmul_mx(
-                        out=z[:],
-                        lhsT=x_codes[:, b * ORDERS + k, t * P : (t + 1) * P].bitcast(FP8X4),
-                        lhsT_scale=x_scales[:, b * ORDERS + k, t * P : (t + 1) * P],
-                        rhs=w_codes[:, r * ORDERS + k, :].bitcast(FP8X4),
-                        rhs_scale=w_scales[:, r * ORDERS + k, :],
-                        start=(k == 0),
-                        stop=(k == ORDERS - 1),
-                    )
+                for i in range(BANK_TILES):
+                    t = j * BANK_TILES + i
+                    for k in range(ORDERS):
+                        nc.tensor.matmul_mx(
+                            out=z[:, i, :],
+                            lhsT=x_codes[:, b * ORDERS + k, t * P : (t + 1) * P].bitcast(FP8X4),
+                            lhsT_scale=x_scales[:, b * ORDERS + k, t * P : (t + 1) * P],
+                            rhs=w_codes[:, r * ORDERS + k, :].bitcast(FP8X4),
+                            rhs_scale=w_scales[:, r * ORDERS + k, :],
+                            start=(k == 0),
+                            stop=(k == ORDERS - 1),
+                        )
             for s in range(ROUND_SETS):
-                for t, z in zip(tiles, banks):
+                for t in range(TILES):
                     row = b * TILES + t
                     col = row * SETS + r * ROUND_SETS + s
                     nc.vector.scalar_tensor_tensor(
-                        out=acc[:, row, :],
-                        in0=z[:, s * OUT : (s + 1) * OUT],
+                        out=acc[:, s % SLOTS, row, :],
+                        in0=banks[t // BANK_TILES][:, t % BANK_TILES, s * OUT : (s + 1) * OUT],
                         scalar=emb_f32[:, col : col + 1],
-                        in1=acc[:, row, :],
+                        in1=acc[:, s % SLOTS, row, :],
                         op0=MULT,
                         op1=ADD,
                     )
 
-        prepare_w(0)
+        def store(b):
+            rows = slice(b * TILES, (b + 1) * TILES)
+            result = stage.tile([P, TILES, OUT], F32, name="result")
+            nc.vector.tensor_add(out=result[:], in0=acc[:, 0, rows, :], in1=acc[:, 1, rows, :])
+            nc.sync.dma_start(
+                out=out[b].rearrange("(p t) o -> p (t o)", t=TILES),
+                in_=result[:].rearrange("p t o -> p (t o)"),
+            )
+
         prepare_x(0)
+        prepare_w(0)
+        bias_term()
         for r in range(ROUNDS):
             for b in range(BATCH):
                 if r == 0 and b + 1 < BATCH:
                     prepare_x(b + 1)
                 if r + 1 < ROUNDS and b == BATCH - 1:
                     prepare_w(r + 1)
-                for pair in range(TILES // 2):
-                    node_tile_pair(r, b, pair)
+                batch_round(r, b)
                 if r == ROUNDS - 1:
-                    nc.sync.dma_start(
-                        out=out[b].rearrange("(p t) o -> p (t o)", t=TILES),
-                        in_=acc[:, b * TILES : (b + 1) * TILES, :].rearrange("p t o -> p (t o)"),
-                    )
+                    store(b)

@@ -36,6 +36,7 @@ def tile_dygcn_pb_kernel(tc, x_g, emb, weights_pool, bias_pool, out):
         stage = ctx.enter_context(tc.tile_pool(name="stage", bufs=3))
         psum_x = ctx.enter_context(tc.psum_pool(name="psum_x", bufs=4))
         psum_z = ctx.enter_context(tc.psum_pool(name="psum_z", bufs=4))
+        ctx.enter_context(tc.manual_schedule())
 
         x_raw = [keep.tile([P, ORDERS * TILES * FEAT], BF16, name="x_raw%d" % b) for b in range(BATCH)]
         w_raw = [keep.tile([P, ORDERS, ROUND_SETS, PACK * OUT], BF16, name="w_raw%d" % r) for r in range(ROUNDS)]
@@ -99,22 +100,25 @@ def tile_dygcn_pb_kernel(tc, x_g, emb, weights_pool, bias_pool, out):
                 )
 
         def prepare_w(r):
+            grouped = [
+                stage.tile([P, ROUND_COLS, PACK], BF16, align_bytes=64, name="w_grouped") for k in range(ORDERS)
+            ]
             for k in range(ORDERS):
-                grouped = stage.tile([P, ROUND_COLS, PACK], BF16, align_bytes=64, name="w_grouped")
                 if k == 0:
                     nc.scalar.copy(
-                        out=grouped[:].rearrange("p (e o) j -> p e o j", o=OUT),
+                        out=grouped[k][:].rearrange("p (e o) j -> p e o j", o=OUT),
                         in_=w_raw[r][:, k, :, :].rearrange("p e (j o) -> p e o j", j=PACK),
                     )
                 else:
                     nc.vector.tensor_copy(
-                        out=grouped[:].rearrange("p (e c i) j -> p e c j i", e=ROUND_SETS, i=4),
+                        out=grouped[k][:].rearrange("p (e c i) j -> p e c j i", e=ROUND_SETS, i=4),
                         in_=w_raw[r][:, k, :, :].rearrange("p e (j c i) -> p e c j i", j=PACK, i=4),
                     )
+            for k in range(ORDERS):
                 nc.vector.quantize_mx(
                     out=w_codes[:, r * ORDERS + k, :].bitcast(FP8X4),
                     scales=w_scales[:, r * ORDERS + k, :],
-                    in_=grouped[:].rearrange("p c j -> p (c j)"),
+                    in_=grouped[k][:].rearrange("p c j -> p (c j)"),
                 )
 
         def prepare_x(b):

@@ -10,6 +10,7 @@ U8 = mybir.dt.uint8
 FP8X4 = mybir.dt.float8_e4m3fn_x4
 MULT = mybir.AluOpType.mult
 ADD = mybir.AluOpType.add
+COPY = mybir.ActivationFunctionType.Copy
 
 P = 128
 PACK = 4
@@ -24,7 +25,7 @@ ROUND_SETS = 4
 ROUNDS = SETS // ROUND_SETS
 ROUND_COLS = ROUND_SETS * OUT
 BANK_TILES = BANK // ROUND_COLS
-SLOTS = 2
+VECTOR_SETS = 2
 
 FLOPS = 2 * BATCH * NODES * ORDERS * FEAT * SETS * OUT
 
@@ -36,7 +37,6 @@ def tile_dygcn_pb_kernel(tc, x_g, emb, weights_pool, bias_pool, out):
         stage = ctx.enter_context(tc.tile_pool(name="stage", bufs=3))
         psum_x = ctx.enter_context(tc.psum_pool(name="psum_x", bufs=4))
         psum_z = ctx.enter_context(tc.psum_pool(name="psum_z", bufs=4))
-        ctx.enter_context(tc.manual_schedule())
 
         x_raw = [keep.tile([P, ORDERS * TILES * FEAT], BF16, name="x_raw%d" % b) for b in range(BATCH)]
         w_raw = [keep.tile([P, ORDERS, ROUND_SETS, PACK * OUT], BF16, name="w_raw%d" % r) for r in range(ROUNDS)]
@@ -44,7 +44,7 @@ def tile_dygcn_pb_kernel(tc, x_g, emb, weights_pool, bias_pool, out):
         x_scales = keep.tile([P, BATCH * ORDERS, TILES * P], U8, align_bytes=64)
         w_codes = keep.tile([P, ROUNDS * ORDERS, ROUND_COLS], U32, align_bytes=64)
         w_scales = keep.tile([P, ROUNDS * ORDERS, ROUND_COLS], U8, align_bytes=64)
-        acc = keep.tile([P, SLOTS, ROWS, OUT], F32)
+        acc = keep.tile([P, ROUND_SETS, ROWS, OUT], F32)
 
         def load_x(b):
             for k in range(ORDERS):
@@ -82,7 +82,7 @@ def tile_dygcn_pb_kernel(tc, x_g, emb, weights_pool, bias_pool, out):
             nc.scalar.dma_start(
                 out=bias_diag[d * SETS : (d + 1) * SETS, d * OUT : (d + 1) * OUT], in_=bias_pool
             )
-        nc.vector.memset(acc[:, 1, :, :], 0.0)
+        nc.vector.memset(acc[:, 1:, :, :], 0.0)
         emb_f32 = keep.tile([P, ROWS * SETS], F32)
         nc.vector.tensor_copy(out=emb_f32[:], in_=emb_bf[:].rearrange("p b c -> p (b c)"))
         emb_t_ps = psum_x.tile([P, GROUPS, P], F32, name="xt")
@@ -100,25 +100,22 @@ def tile_dygcn_pb_kernel(tc, x_g, emb, weights_pool, bias_pool, out):
                 )
 
         def prepare_w(r):
-            grouped = [
-                stage.tile([P, ROUND_COLS, PACK], BF16, align_bytes=64, name="w_grouped") for k in range(ORDERS)
-            ]
             for k in range(ORDERS):
+                grouped = stage.tile([P, ROUND_COLS, PACK], BF16, align_bytes=64, name="w_grouped")
                 if k == 0:
                     nc.scalar.copy(
-                        out=grouped[k][:].rearrange("p (e o) j -> p e o j", o=OUT),
+                        out=grouped[:].rearrange("p (e o) j -> p e o j", o=OUT),
                         in_=w_raw[r][:, k, :, :].rearrange("p e (j o) -> p e o j", j=PACK),
                     )
                 else:
                     nc.vector.tensor_copy(
-                        out=grouped[k][:].rearrange("p (e c i) j -> p e c j i", e=ROUND_SETS, i=4),
+                        out=grouped[:].rearrange("p (e c i) j -> p e c j i", e=ROUND_SETS, i=4),
                         in_=w_raw[r][:, k, :, :].rearrange("p e (j c i) -> p e c j i", j=PACK, i=4),
                     )
-            for k in range(ORDERS):
                 nc.vector.quantize_mx(
                     out=w_codes[:, r * ORDERS + k, :].bitcast(FP8X4),
                     scales=w_scales[:, r * ORDERS + k, :],
-                    in_=grouped[k][:].rearrange("p c j -> p (c j)"),
+                    in_=grouped[:].rearrange("p c j -> p (c j)"),
                 )
 
         def prepare_x(b):
@@ -144,43 +141,47 @@ def tile_dygcn_pb_kernel(tc, x_g, emb, weights_pool, bias_pool, out):
                     in_=grouped[:],
                 )
 
-        def batch_round(r, b):
-            banks = []
-            for j in range(TILES // BANK_TILES):
-                z = psum_z.tile([P, BANK_TILES, ROUND_COLS], F32, name="z")
-                banks.append(z)
-                for i in range(BANK_TILES):
-                    t = j * BANK_TILES + i
-                    for k in range(ORDERS):
-                        nc.tensor.matmul_mx(
-                            out=z[:, i, :],
-                            lhsT=x_codes[:, b * ORDERS + k, t * P : (t + 1) * P].bitcast(FP8X4),
-                            lhsT_scale=x_scales[:, b * ORDERS + k, t * P : (t + 1) * P],
-                            rhs=w_codes[:, r * ORDERS + k, :].bitcast(FP8X4),
-                            rhs_scale=w_scales[:, r * ORDERS + k, :],
-                            start=(k == 0),
-                            stop=(k == ORDERS - 1),
-                        )
-            for s in range(ROUND_SETS):
-                for t in range(TILES):
-                    row = b * TILES + t
-                    col = row * SETS + r * ROUND_SETS + s
-                    nc.vector.scalar_tensor_tensor(
-                        out=acc[:, s % SLOTS, row, :],
-                        in0=banks[t // BANK_TILES][:, t % BANK_TILES, s * OUT : (s + 1) * OUT],
-                        scalar=emb_f32[:, col : col + 1],
-                        in1=acc[:, s % SLOTS, row, :],
-                        op0=MULT,
-                        op1=ADD,
+        def bank_round(r, b, j):
+            rows = slice(b * TILES + j * BANK_TILES, b * TILES + (j + 1) * BANK_TILES)
+            z = psum_z.tile([P, BANK_TILES, ROUND_COLS], F32, name="z")
+            for i in range(BANK_TILES):
+                t = j * BANK_TILES + i
+                for k in range(ORDERS):
+                    nc.tensor.matmul_mx(
+                        out=z[:, i, :],
+                        lhsT=x_codes[:, b * ORDERS + k, t * P : (t + 1) * P].bitcast(FP8X4),
+                        lhsT_scale=x_scales[:, b * ORDERS + k, t * P : (t + 1) * P],
+                        rhs=w_codes[:, r * ORDERS + k, :].bitcast(FP8X4),
+                        rhs_scale=w_scales[:, r * ORDERS + k, :],
+                        start=(k == 0),
+                        stop=(k == ORDERS - 1),
                     )
+            scaled = stage.tile([P, ROUND_SETS - VECTOR_SETS, BANK_TILES, OUT], F32, name="scaled")
+            for i in range(BANK_TILES):
+                row = b * TILES + j * BANK_TILES + i
+                for s in range(ROUND_SETS):
+                    col = row * SETS + r * ROUND_SETS + s
+                    weight = emb_f32[:, col : col + 1]
+                    z_set = z[:, i, s * OUT : (s + 1) * OUT]
+                    if s < VECTOR_SETS:
+                        nc.vector.scalar_tensor_tensor(
+                            out=acc[:, s, row, :], in0=z_set, scalar=weight, in1=acc[:, s, row, :], op0=MULT, op1=ADD
+                        )
+                    else:
+                        nc.scalar.activation(out=scaled[:, s - VECTOR_SETS, i, :], in_=z_set, func=COPY, scale=weight)
+            nc.gpsimd.tensor_tensor(
+                out=acc[:, VECTOR_SETS:, rows, :], in0=acc[:, VECTOR_SETS:, rows, :], in1=scaled[:], op=ADD
+            )
 
-        def store(b):
-            rows = slice(b * TILES, (b + 1) * TILES)
-            result = stage.tile([P, TILES, OUT], F32, name="result")
-            nc.vector.tensor_add(out=result[:], in0=acc[:, 0, rows, :], in1=acc[:, 1, rows, :])
+        def store(b, j):
+            rows = slice(b * TILES + j * BANK_TILES, b * TILES + (j + 1) * BANK_TILES)
+            result = stage.tile([P, BANK_TILES * OUT], F32, name="result")
+            nc.vector.tensor_reduce(
+                out=result[:], in_=acc[:, :, rows, :].rearrange("p s t o -> p (t o) s"), axis=mybir.AxisListType.X, op=ADD
+            )
             nc.sync.dma_start(
-                out=out[b].rearrange("(p t) o -> p (t o)", t=TILES),
-                in_=result[:].rearrange("p t o -> p (t o)"),
+                out=out[b].rearrange("(p t) o -> p t o", t=TILES)[:, j * BANK_TILES : (j + 1) * BANK_TILES, :],
+                in_=result[:].rearrange("p (t o) -> p t o", o=OUT),
             )
 
         prepare_x(0)
@@ -192,6 +193,7 @@ def tile_dygcn_pb_kernel(tc, x_g, emb, weights_pool, bias_pool, out):
                     prepare_x(b + 1)
                 if r + 1 < ROUNDS and b == BATCH - 1:
                     prepare_w(r + 1)
-                batch_round(r, b)
-                if r == ROUNDS - 1:
-                    store(b)
+                for j in range(TILES // BANK_TILES):
+                    bank_round(r, b, j)
+                    if r == ROUNDS - 1:
+                        store(b, j)

from contextlib import ExitStack

import concourse.mybir as mybir
from concourse.masks import make_identity

BF16 = mybir.dt.bfloat16
F32 = mybir.dt.float32
U32 = mybir.dt.uint32
U8 = mybir.dt.uint8
FP8X4 = mybir.dt.float8_e4m3fn_x4
MULT = mybir.AluOpType.mult
ADD = mybir.AluOpType.add
COPY = mybir.ActivationFunctionType.Copy

P = 128
PACK = 4
BATCH, ORDERS, NODES, FEAT = 4, 3, 512, 512
SETS, OUT = 16, 64
TILES = NODES // P
ROWS = BATCH * TILES
HALVES = 2
WORDS = FEAT // 2
BANK = 512
ROUND_SETS = 4
ROUNDS = SETS // ROUND_SETS
ROUND_COLS = ROUND_SETS * OUT
BANK_TILES = BANK // ROUND_COLS
VECTOR_SETS = 2

FLOPS = 2 * BATCH * NODES * ORDERS * FEAT * SETS * OUT


def tile_dygcn_pb_kernel(tc, x_g, emb, weights_pool, bias_pool, out):
    nc = tc.nc
    with ExitStack() as ctx:
        keep = ctx.enter_context(tc.tile_pool(name="keep", bufs=1))
        stage = ctx.enter_context(tc.tile_pool(name="stage", bufs=3))
        psum_x = ctx.enter_context(tc.psum_pool(name="psum_x", bufs=4))
        psum_z = ctx.enter_context(tc.psum_pool(name="psum_z", bufs=4))

        x_raw = [keep.tile([P, ORDERS * TILES * FEAT], BF16, name="x_raw%d" % b) for b in range(BATCH)]
        w_raw = [keep.tile([P, ORDERS, ROUND_SETS, PACK * OUT], BF16, name="w_raw%d" % r) for r in range(ROUNDS)]
        x_codes = keep.tile([P, BATCH * ORDERS, TILES * P], U32, align_bytes=64)
        x_scales = keep.tile([P, BATCH * ORDERS, TILES * P], U8, align_bytes=64)
        w_codes = keep.tile([P, ROUNDS * ORDERS, ROUND_COLS], U32, align_bytes=64)
        w_scales = keep.tile([P, ROUNDS * ORDERS, ROUND_COLS], U8, align_bytes=64)
        acc = keep.tile([P, ROUND_SETS, ROWS, OUT], F32)

        def load_x(b):
            for k in range(ORDERS):
                nc.sync.dma_start(
                    out=x_raw[b][:, k * TILES * FEAT : (k + 1) * TILES * FEAT],
                    in_=x_g[b, k].rearrange("(p t) f -> p (t f)", t=TILES),
                )

        def load_w(r):
            for k in range(ORDERS):
                for u in range(HALVES):
                    nc.sync.dma_start(
                        out=w_raw[r][:, k, :, u * 2 * OUT : (u + 1) * 2 * OUT],
                        in_=weights_pool[
                            r * ROUND_SETS : (r + 1) * ROUND_SETS, k, u * 2 * P : (u + 1) * 2 * P, :
                        ].rearrange("e (p c) o -> p e (c o)", c=2),
                    )

        load_x(0)
        load_w(0)
        for b in range(1, BATCH):
            load_x(b)
        for r in range(1, ROUNDS):
            load_w(r)

        ident = keep.tile([P, P], F32)
        make_identity(nc, ident[:])
        emb_bf = keep.tile([P, BATCH, TILES * SETS], BF16)
        nc.scalar.dma_start(out=emb_bf[:], in_=emb.rearrange("b (p t) e -> p b (t e)", t=TILES))
        DIAG = P // SETS
        GROUPS = ROWS // DIAG
        bias_diag = keep.tile([P, DIAG * OUT], BF16)
        nc.vector.memset(bias_diag[:], 0.0)
        for d in range(DIAG):
            nc.scalar.dma_start(
                out=bias_diag[d * SETS : (d + 1) * SETS, d * OUT : (d + 1) * OUT], in_=bias_pool
            )
        nc.vector.memset(acc[:, 1:, :, :], 0.0)
        emb_f32 = keep.tile([P, ROWS * SETS], F32)
        nc.vector.tensor_copy(out=emb_f32[:], in_=emb_bf[:].rearrange("p b c -> p (b c)"))
        emb_t_ps = psum_x.tile([P, GROUPS, P], F32, name="xt")
        for g in range(GROUPS):
            nc.tensor.transpose(emb_t_ps[:, g, :], emb_f32[:, g * P : (g + 1) * P], ident[:])
        emb_t = keep.tile([P, GROUPS, P], BF16)
        nc.vector.tensor_copy(out=emb_t[:], in_=emb_t_ps[:])

        def bias_term():
            for g in range(GROUPS):
                bias_ps = psum_z.tile([P, DIAG * OUT], F32, name="z")
                nc.tensor.matmul(bias_ps[:], lhsT=emb_t[:, g, :], rhs=bias_diag[:], start=True, stop=True)
                nc.scalar.copy(
                    out=acc[:, 0, g * DIAG : (g + 1) * DIAG, :].rearrange("p d o -> p (d o)"), in_=bias_ps[:]
                )

        def prepare_w(r):
            for k in range(ORDERS):
                grouped = stage.tile([P, ROUND_COLS, PACK], BF16, align_bytes=64, name="w_grouped")
                if k == 0:
                    nc.scalar.copy(
                        out=grouped[:].rearrange("p (e o) j -> p e o j", o=OUT),
                        in_=w_raw[r][:, k, :, :].rearrange("p e (j o) -> p e o j", j=PACK),
                    )
                else:
                    nc.vector.tensor_copy(
                        out=grouped[:].rearrange("p (e c i) j -> p e c j i", e=ROUND_SETS, i=4),
                        in_=w_raw[r][:, k, :, :].rearrange("p e (j c i) -> p e c j i", j=PACK, i=4),
                    )
                nc.vector.quantize_mx(
                    out=w_codes[:, r * ORDERS + k, :].bitcast(FP8X4),
                    scales=w_scales[:, r * ORDERS + k, :],
                    in_=grouped[:].rearrange("p c j -> p (c j)"),
                )

        def prepare_x(b):
            x_words = x_raw[b][:].bitcast(F32)
            for k in range(ORDERS):
                grouped = stage.tile([P, TILES * P * PACK], BF16, align_bytes=64, name="x_grouped")
                grouped_words = grouped[:].bitcast(F32).rearrange("p (t n u) -> p t n u", t=TILES, u=HALVES)
                for pair in range(TILES // 2):
                    xt = psum_x.tile([P, 2, HALVES, P], F32, name="xt")
                    for i in range(2):
                        row = (k * TILES + 2 * pair + i) * WORDS
                        for u in range(HALVES):
                            nc.tensor.transpose(
                                xt[:, i, u, :], x_words[:, row + u * P : row + (u + 1) * P], ident[:]
                            )
                    nc.scalar.copy(
                        out=grouped_words[:, 2 * pair : 2 * pair + 2, :, :],
                        in_=xt[:].rearrange("p i u n -> p i n u"),
                    )
                nc.vector.quantize_mx(
                    out=x_codes[:, b * ORDERS + k, :].bitcast(FP8X4),
                    scales=x_scales[:, b * ORDERS + k, :],
                    in_=grouped[:],
                )

        def bank_round(r, b, j):
            rows = slice(b * TILES + j * BANK_TILES, b * TILES + (j + 1) * BANK_TILES)
            z = psum_z.tile([P, BANK_TILES, ROUND_COLS], F32, name="z")
            for i in range(BANK_TILES):
                t = j * BANK_TILES + i
                for k in range(ORDERS):
                    nc.tensor.matmul_mx(
                        out=z[:, i, :],
                        lhsT=x_codes[:, b * ORDERS + k, t * P : (t + 1) * P].bitcast(FP8X4),
                        lhsT_scale=x_scales[:, b * ORDERS + k, t * P : (t + 1) * P],
                        rhs=w_codes[:, r * ORDERS + k, :].bitcast(FP8X4),
                        rhs_scale=w_scales[:, r * ORDERS + k, :],
                        start=(k == 0),
                        stop=(k == ORDERS - 1),
                    )
            scaled = stage.tile([P, ROUND_SETS - VECTOR_SETS, BANK_TILES, OUT], F32, name="scaled")
            for i in range(BANK_TILES):
                row = b * TILES + j * BANK_TILES + i
                for s in range(ROUND_SETS):
                    col = row * SETS + r * ROUND_SETS + s
                    weight = emb_f32[:, col : col + 1]
                    z_set = z[:, i, s * OUT : (s + 1) * OUT]
                    if s < VECTOR_SETS:
                        nc.vector.scalar_tensor_tensor(
                            out=acc[:, s, row, :], in0=z_set, scalar=weight, in1=acc[:, s, row, :], op0=MULT, op1=ADD
                        )
                    else:
                        nc.scalar.activation(out=scaled[:, s - VECTOR_SETS, i, :], in_=z_set, func=COPY, scale=weight)
            nc.gpsimd.tensor_tensor(
                out=acc[:, VECTOR_SETS:, rows, :], in0=acc[:, VECTOR_SETS:, rows, :], in1=scaled[:], op=ADD
            )

        def store(b, j):
            rows = slice(b * TILES + j * BANK_TILES, b * TILES + (j + 1) * BANK_TILES)
            result = stage.tile([P, BANK_TILES * OUT], F32, name="result")
            nc.vector.tensor_reduce(
                out=result[:], in_=acc[:, :, rows, :].rearrange("p s t o -> p (t o) s"), axis=mybir.AxisListType.X, op=ADD
            )
            nc.sync.dma_start(
                out=out[b].rearrange("(p t) o -> p t o", t=TILES)[:, j * BANK_TILES : (j + 1) * BANK_TILES, :],
                in_=result[:].rearrange("p (t o) -> p t o", o=OUT),
            )

        prepare_x(0)
        prepare_w(0)
        bias_term()
        for r in range(ROUNDS):
            for b in range(BATCH):
                if r == 0 and b + 1 < BATCH:
                    prepare_x(b + 1)
                if r + 1 < ROUNDS and b == BATCH - 1:
                    prepare_w(r + 1)
                for j in range(TILES // BANK_TILES):
                    bank_round(r, b, j)
                    if r == ROUNDS - 1:
                        store(b, j)
